import numpy as np
import ml_dtypes


def mxq(x, axis, fmt="e4m3"):
    dtype, down = {"e4m3": (ml_dtypes.float8_e4m3fn, 7), "e5m2": (ml_dtypes.float8_e5m2, 14)}[fmt]
    v = np.moveaxis(np.asarray(x, np.float32).astype(ml_dtypes.bfloat16).astype(np.float64), axis, -1)
    blocks = v.reshape(v.shape[:-1] + (-1, 32))
    amax = np.abs(blocks).max(-1, keepdims=True)
    byte = np.maximum(np.where(amax > 0, np.frexp(amax)[1] - 1 + 127, 0) - down, 1)
    scale = np.exp2(byte - 127.0)
    codes = (blocks / scale).astype(np.float32).astype(dtype).astype(np.float64)
    return np.moveaxis((codes * scale).reshape(v.shape), -1, axis)


WIDE = False


def mx_kscale(k):
    if not WIDE:
        return np.ones(k)
    levels = np.array([10, -10, 5, -5, 0])
    a = np.random.permutation(np.resize(levels, k // 512 * 4)).reshape(k // 512, 4)
    idx = np.arange(k)
    return np.exp2(a[idx // 512, idx % 128 // 32])


BF16 = ml_dtypes.bfloat16


def bf(x):
    return np.asarray(x, np.float32).astype(BF16)


def f64(x):
    return np.asarray(x).astype(np.float64)


E2M1 = np.array([0.0, 0.5, 1.0, 1.5, 2.0, 3.0, 4.0, 6.0, -0.0, -0.5, -1.0, -1.5, -2.0, -3.0, -4.0, -6.0])


def pack_weight(w, fmt):
    k, n = w.shape
    w = f64(bf(w)).reshape(k // 32, 32, n)
    amax = np.abs(w).max(1)
    if fmt == "e4m3":
        byte = np.frexp(amax)[1] - 1 + 127 - 7
    else:
        mant, ex = np.frexp(amax / 6.0)
        byte = np.where(mant > 0.5, ex, ex - 1) + 127
    byte = np.clip(np.where(amax > 0, byte, 1), 1, 254)
    scaled = (w * np.exp2(127.0 - byte)[:, None, :]).reshape(k, n).astype(np.float32)
    by_word = np.ascontiguousarray(scaled.reshape(k // 512, 128, 4, n).transpose(0, 1, 3, 2))
    if fmt == "e4m3":
        words = by_word.astype(ml_dtypes.float8_e4m3fn).view(np.uint8)
    else:
        c = by_word.astype(ml_dtypes.float4_e2m1fn).view(np.uint8) & 0xF
        words = c[..., 0::2] | (c[..., 1::2] << 4)
    return np.ascontiguousarray(words), np.ascontiguousarray(byte.astype(np.uint8).reshape(k // 512, 16, n))


def unpack_weight(words, scales, fmt):
    g, p, n, _ = words.shape
    if fmt == "e4m3":
        vals = np.ascontiguousarray(words).view(ml_dtypes.float8_e4m3fn).astype(np.float64)
    else:
        nib = np.empty((g, p, n, 4), np.uint8)
        nib[..., 0::2] = words & 0xF
        nib[..., 1::2] = words >> 4
        vals = E2M1[nib]
    vals = vals * np.repeat(np.exp2(scales.astype(np.float64) - 127.0), 8, axis=1)[..., None]
    return vals.transpose(0, 1, 3, 2).reshape(g * 512, n)


B, L, C, H, DH, AX = 2, 64, 16384, 16, 96, 3
D3 = DH // AX
HALF = D3 // 2
ROPE_BASE = 10000.0
COORD_MAX = 10.0


def rope_3d(x, coords):
    inv_freq = 1.0 / (ROPE_BASE ** (np.arange(HALF) / HALF))
    ang = coords[..., None] * inv_freq
    cos = np.cos(ang)[:, None]
    sin = np.sin(ang)[:, None]
    xr = x.reshape(B, H, L, AX, D3)
    x1, x2 = xr[..., :HALF], xr[..., HALF:]
    out = np.concatenate([x1 * cos - x2 * sin, x1 * sin + x2 * cos], axis=-1)
    return out.reshape(B, H, L, DH)


def setup_inputs():
    s = mx_kscale(C)
    x_in = bf(np.random.standard_normal((B, L, C)) * s)
    coords = bf(np.random.uniform(size=(B, L, AX)) * COORD_MAX)
    w = np.random.standard_normal((H * DH, C)) * 1.5 / np.sqrt(C) / s
    words, scales = pack_weight(np.ascontiguousarray(w.T), "e4m3")
    return {"x_in": x_in,
            "coords": coords,
            "w_words": words,
            "w_scales": scales}


def reference(x_in, coords, w_words, w_scales):
    p = mxq(f64(x_in), 2, "e4m3") @ unpack_weight(w_words, w_scales, "e4m3")
    p = p.reshape(B, L, H, DH).transpose(0, 2, 1, 3)
    return rope_3d(p, f64(coords))

@@ -1,0 +1,210 @@
+import math
+from contextlib import ExitStack
+
+import concourse.mybir as mybir
+from concourse.masks import make_identity
+
+F32 = mybir.dt.float32
+BF16 = mybir.dt.bfloat16
+I32 = mybir.dt.int32
+U32 = mybir.dt.uint32
+U8 = mybir.dt.uint8
+FP8X4 = mybir.dt.float8_e4m3fn_x4
+ALU = mybir.AluOpType
+ACT = mybir.ActivationFunctionType
+
+P = 128
+BATCH, TOKENS_PER_BATCH = 2, 64
+K = 16384
+K_PASS = 512
+GROUPS = K // K_PASS
+HEADS, HEAD_DIM, AXES = 16, 96, 3
+BLOCK = HEAD_DIM // AXES
+HALF = BLOCK // 2
+N = HEADS * HEAD_DIM
+BANK = 512
+BANKS = N // BANK
+ROPE_BASE = 10000.0
+
+X_CHUNK_GROUPS = 8
+X_CHUNKS = GROUPS // X_CHUNK_GROUPS
+WORDS_PER_GROUP = K_PASS // 2
+QUANT_GROUPS = 4
+PLANES_PER_TILE = 4
+QUADS = GROUPS // PLANES_PER_TILE
+LAST_GROUPS = 4
+W_BUFS = 8
+TABLE_REPEATS = 6
+
+FLOPS = 2 * P * K * N
+
+
+def tile_crossattnrope_pa_k_kernel(tc, x_in, coords, w_words, w_scales, out):
+    nc = tc.nc
+    x_rows = x_in.rearrange("b l k -> (b l) k")
+
+    with ExitStack() as stack:
+        const = stack.enter_context(tc.tile_pool(name="const", bufs=1))
+        x_pool = stack.enter_context(tc.tile_pool(name="x_pool", bufs=X_CHUNKS))
+        grouped_pool = stack.enter_context(tc.tile_pool(name="grouped_pool", bufs=3))
+        w_pool = stack.enter_context(tc.tile_pool(name="w_pool", bufs=W_BUFS))
+        rope_pool = stack.enter_context(tc.tile_pool(name="rope_pool", bufs=2))
+        acc_pool = stack.enter_context(tc.psum_pool(name="acc_pool", bufs=1))
+        xt_pool = stack.enter_context(tc.psum_pool(name="xt_pool", bufs=4))
+        stack.enter_context(tc.manual_schedule())
+
+        x_chunks = []
+        for chunk in range(X_CHUNKS):
+            x_sb = x_pool.tile([P, X_CHUNK_GROUPS * K_PASS], BF16, name="x_sb")
+            k0 = chunk * X_CHUNK_GROUPS * K_PASS
+            nc.sync.dma_start(out=x_sb[:], in_=x_rows[:, k0 : k0 + X_CHUNK_GROUPS * K_PASS])
+            x_chunks.append(x_sb)
+        coords_sb = const.tile([P, AXES], BF16)
+        nc.scalar.dma_start(out=coords_sb[:], in_=coords.rearrange("b l a -> (b l) a"))
+
+        w_planes = const.tile([P, QUADS, N], U8, align_bytes=64)
+        nc.vector.memset(w_planes[:].rearrange("p u n -> p (u n)").bitcast(I32), 0)
+        for quad in range(QUADS):
+            g0 = quad * PLANES_PER_TILE
+            for quarter in range(4):
+                nc.sync.dma_start(
+                    out=w_planes[32 * quarter : 32 * quarter + 16, quad, :].bitcast(I32),
+                    in_=w_scales[g0 : g0 + PLANES_PER_TILE, 4 * quarter : 4 * quarter + 4, :].bitcast(I32),
+                )
+
+        identity = const.tile([P, P], F32)
+        make_identity(nc, identity[:])
+
+        angle = const.tile([P, 2, AXES, HALF], F32)
+        for i in range(HALF):
+            nc.vector.tensor_scalar(
+                out=angle[:, 1, :, i], in0=coords_sb[:], scalar1=ROPE_BASE ** (-i / HALF), scalar2=None, op0=ALU.mult
+            )
+        nc.vector.tensor_scalar_add(out=angle[:, 0], in0=angle[:, 1], scalar1=math.pi / 2)
+        angle_flat = angle[:].rearrange("p s a i -> p (s a i)")
+        turns_int = const.tile([P, 2 * AXES * HALF], I32)
+        nc.vector.tensor_scalar(
+            out=turns_int[:], in0=angle_flat, scalar1=1.0 / (2 * math.pi), scalar2=None, op0=ALU.mult
+        )
+        turns = const.tile([P, 2 * AXES * HALF], F32)
+        nc.vector.tensor_copy(out=turns[:], in_=turns_int[:])
+        reduced = const.tile([P, 2 * AXES * HALF], F32)
+        nc.vector.scalar_tensor_tensor(
+            out=reduced[:], in0=turns[:], scalar=-2 * math.pi, in1=angle_flat, op0=ALU.mult, op1=ALU.add
+        )
+        above = const.tile([P, 2 * AXES * HALF], F32)
+        nc.vector.tensor_scalar(
+            out=above[:], in0=reduced[:], scalar1=math.pi, scalar2=-2 * math.pi, op0=ALU.is_gt, op1=ALU.mult
+        )
+        below = const.tile([P, 2 * AXES * HALF], F32)
+        nc.vector.tensor_scalar(
+            out=below[:], in0=reduced[:], scalar1=-math.pi, scalar2=2 * math.pi, op0=ALU.is_lt, op1=ALU.mult
+        )
+        nc.vector.tensor_add(out=above[:], in0=above[:], in1=below[:])
+        wrapped = const.tile([P, 2, AXES, HALF], F32)
+        nc.vector.tensor_add(out=wrapped[:].rearrange("p s a i -> p (s a i)"), in0=reduced[:], in1=above[:])
+
+        cos_table = const.tile([P, TABLE_REPEATS, AXES, 2, HALF], F32)
+        sin_table = const.tile([P, TABLE_REPEATS, AXES, 2, HALF], F32)
+        table_shape = [P, TABLE_REPEATS, AXES, HALF]
+        for_cos = wrapped[:, 0].unsqueeze(1).to_broadcast(table_shape)
+        for_sin = wrapped[:, 1].unsqueeze(1).to_broadcast(table_shape)
+        nc.scalar.activation(out=cos_table[:, :, :, 0, :], in_=for_cos, func=ACT.Sin)
+        nc.scalar.activation(out=cos_table[:, :, :, 1, :], in_=for_cos, func=ACT.Sin)
+        nc.scalar.activation(out=sin_table[:, :, :, 0, :], in_=for_sin, func=ACT.Sin, scale=-1.0)
+        nc.scalar.activation(out=sin_table[:, :, :, 1, :], in_=for_sin, func=ACT.Sin)
+        cos_flat = cos_table[:].rearrange("p r a h i -> p (r a h i)")
+        sin_flat = sin_table[:].rearrange("p r a h i -> p (r a h i)")
+
+        x_codes = const.tile([P, GROUPS * P], U32, align_bytes=64)
+        x_scales = const.tile([P, GROUPS * P], U8, align_bytes=64)
+        groups_per_bank = BANK // (2 * P)
+        for chunk in range(X_CHUNKS):
+            x_words = x_chunks[chunk][:].bitcast(F32)
+            for call in range(X_CHUNK_GROUPS // QUANT_GROUPS):
+                grouped = grouped_pool.tile([P, QUANT_GROUPS * P * 4], BF16, align_bytes=64)
+                grouped_words = grouped[:].bitcast(F32)
+                for bank in range(QUANT_GROUPS // groups_per_bank):
+                    xt = xt_pool.tile([P, groups_per_bank, 2, P], F32)
+                    for j in range(groups_per_bank):
+                        w0 = ((call * QUANT_GROUPS) + bank * groups_per_bank + j) * WORDS_PER_GROUP
+                        for u in range(2):
+                            nc.tensor.transpose(
+                                xt[:, j, u, :], x_words[:, w0 + u : w0 + WORDS_PER_GROUP : 2], identity[:]
+                            )
+                    side_by_side = grouped_words[:, bank * BANK : (bank + 1) * BANK].rearrange(
+                        "p (j r u) -> p j r u", j=groups_per_bank, u=2
+                    )
+                    if call == 0 and bank == 0:
+                        nc.vector.tensor_copy(out=side_by_side, in_=xt[:].rearrange("p j u r -> p j r u"))
+                    else:
+                        nc.scalar.copy(out=side_by_side, in_=xt[:].rearrange("p j u r -> p j r u"))
+                c0 = (chunk * X_CHUNK_GROUPS + call * QUANT_GROUPS) * P
+                nc.vector.quantize_mx(
+                    out=x_codes[:, c0 : c0 + QUANT_GROUPS * P].bitcast(FP8X4),
+                    scales=x_scales[:, c0 : c0 + QUANT_GROUPS * P],
+                    in_=grouped[:],
+                )
+
+        acc = [acc_pool.tile([P, BANK], F32, name="acc%d" % bank) for bank in range(BANKS)]
+
+        def mx_pass(group, bank, w_codes):
+            quad, plane = divmod(group, PLANES_PER_TILE)
+            nc.tensor.matmul_mx(
+                out=acc[bank][:],
+                lhsT=x_codes[:, group * P : (group + 1) * P].bitcast(FP8X4),
+                lhsT_scale=x_scales[:, group * P : (group + 1) * P],
+                rhs=w_codes.bitcast(FP8X4),
+                rhs_scale=w_planes[4 * plane : P, quad, bank * BANK : (bank + 1) * BANK],
+                start=(group == 0),
+                stop=(group == GROUPS - 1),
+            )
+
+        for group in range(GROUPS - LAST_GROUPS):
+            w_group = w_pool.tile([P, N], U32, align_bytes=64)
+            nc.sync.dma_start(out=w_group[:].bitcast(I32), in_=w_words[group].rearrange("p n t -> p (n t)").bitcast(I32))
+            for bank in range(BANKS):
+                mx_pass(group, bank, w_group[:, bank * BANK : (bank + 1) * BANK])
+
+        first_last = GROUPS - LAST_GROUPS
+        w_last = []
+        for bank in range(BANKS):
+            w_bank = const.tile([P, LAST_GROUPS, BANK], U32, name="w_bank%d" % bank, align_bytes=64)
+            nc.sync.dma_start(
+                out=w_bank[:].bitcast(I32),
+                in_=w_words[first_last:GROUPS, :, bank * BANK : (bank + 1) * BANK, :]
+                .rearrange("g p n t -> p g (n t)")
+                .bitcast(I32),
+            )
+            w_last.append(w_bank)
+
+        rotated = const.tile([P, N], F32)
+        heads_stored = 0
+        for bank in range(BANKS):
+            for j in range(LAST_GROUPS):
+                mx_pass(first_last + j, bank, w_last[bank][:, j, :])
+
+            t0 = bank * BLOCK
+            by_half = "p (k h i) -> p k h i"
+            acc_halves = acc[bank][:].rearrange(by_half, h=2, i=HALF)
+            sin_halves = sin_flat[:, t0 : t0 + BANK].rearrange(by_half, h=2, i=HALF)
+            own = rope_pool.tile([P, BANK], F32)
+            partner = rope_pool.tile([P, BANK], F32)
+            partner_halves = partner[:].rearrange(by_half, h=2, i=HALF)
+            nc.vector.tensor_mul(out=own[:], in0=acc[bank][:], in1=cos_flat[:, t0 : t0 + BANK])
+            for h in range(2):
+                nc.vector.tensor_mul(
+                    out=partner_halves[:, :, h, :], in0=acc_halves[:, :, 1 - h, :], in1=sin_halves[:, :, h, :]
+                )
+            nc.vector.tensor_add(out=rotated[:, bank * BANK : (bank + 1) * BANK], in0=own[:], in1=partner[:])
+
+            heads_done = (bank + 1) * BANK // HEAD_DIM
+            for b in range(BATCH):
+                rows = slice(b * TOKENS_PER_BATCH, (b + 1) * TOKENS_PER_BATCH)
+                nc.scalar.dma_start(
+                    out=out[b, heads_stored:heads_done].rearrange("h l d -> l h d"),
+                    in_=rotated[rows, heads_stored * HEAD_DIM : heads_done * HEAD_DIM].rearrange(
+                        "l (h d) -> l h d", d=HEAD_DIM
+                    ),
+                )
+            heads_stored = heads_done

@@ -23,7 +23,6 @@ BLOCK = HEAD_DIM // AXES
 HALF = BLOCK // 2
 N = HEADS * HEAD_DIM
 BANK = 512
-BANKS = N // BANK
 ROPE_BASE = 10000.0
 
 X_CHUNK_GROUPS = 8
@@ -32,7 +31,9 @@ WORDS_PER_GROUP = K_PASS // 2
 QUANT_GROUPS = 4
 PLANES_PER_TILE = 4
 QUADS = GROUPS // PLANES_PER_TILE
-LAST_GROUPS = 4
+LAST_GROUPS = 8
+UNITS = ((0, 512), (512, 512), (1024, 256), (1280, 256))
+LAST_PIECES = ((0, 1024, (2, 2, 2, 1, 1)), (1024, 256, (4, 4)), (1280, 256, (4, 3, 1)))
 W_BUFS = 8
 TABLE_REPEATS = 6
 
@@ -48,7 +49,7 @@ def tile_crossattnrope_pa_k_kernel(tc, x_in, coords, w_words, w_scales, out):
         x_pool = stack.enter_context(tc.tile_pool(name="x_pool", bufs=X_CHUNKS))
         grouped_pool = stack.enter_context(tc.tile_pool(name="grouped_pool", bufs=3))
         w_pool = stack.enter_context(tc.tile_pool(name="w_pool", bufs=W_BUFS))
-        rope_pool = stack.enter_context(tc.tile_pool(name="rope_pool", bufs=2))
+        rope_pool = stack.enter_context(tc.tile_pool(name="rope_pool", bufs=len(UNITS)))
         acc_pool = stack.enter_context(tc.psum_pool(name="acc_pool", bufs=1))
         xt_pool = stack.enter_context(tc.psum_pool(name="xt_pool", bufs=4))
         stack.enter_context(tc.manual_schedule())
@@ -146,65 +147,77 @@ def tile_crossattnrope_pa_k_kernel(tc, x_in, coords, w_words, w_scales, out):
                     in_=grouped[:],
                 )
 
-        acc = [acc_pool.tile([P, BANK], F32, name="acc%d" % bank) for bank in range(BANKS)]
+        acc = [acc_pool.tile([P, BANK], F32, name="acc%d" % unit) for unit in range(len(UNITS))]
 
-        def mx_pass(group, bank, w_codes):
+        def mx_pass(group, unit, w_codes):
             quad, plane = divmod(group, PLANES_PER_TILE)
+            c0, width = UNITS[unit]
             nc.tensor.matmul_mx(
-                out=acc[bank][:],
+                out=acc[unit][:, :width],
                 lhsT=x_codes[:, group * P : (group + 1) * P].bitcast(FP8X4),
                 lhsT_scale=x_scales[:, group * P : (group + 1) * P],
                 rhs=w_codes.bitcast(FP8X4),
-                rhs_scale=w_planes[4 * plane : P, quad, bank * BANK : (bank + 1) * BANK],
+                rhs_scale=w_planes[4 * plane : P, quad, c0 : c0 + width],
                 start=(group == 0),
                 stop=(group == GROUPS - 1),
             )
 
-        for group in range(GROUPS - LAST_GROUPS):
+        first_last = GROUPS - LAST_GROUPS
+        for group in range(first_last):
             w_group = w_pool.tile([P, N], U32, align_bytes=64)
             nc.sync.dma_start(out=w_group[:].bitcast(I32), in_=w_words[group].rearrange("p n t -> p (n t)").bitcast(I32))
-            for bank in range(BANKS):
-                mx_pass(group, bank, w_group[:, bank * BANK : (bank + 1) * BANK])
+            for unit, (c0, width) in enumerate(UNITS):
+                mx_pass(group, unit, w_group[:, c0 : c0 + width])
 
-        first_last = GROUPS - LAST_GROUPS
         w_last = []
-        for bank in range(BANKS):
-            w_bank = const.tile([P, LAST_GROUPS, BANK], U32, name="w_bank%d" % bank, align_bytes=64)
-            nc.sync.dma_start(
-                out=w_bank[:].bitcast(I32),
-                in_=w_words[first_last:GROUPS, :, bank * BANK : (bank + 1) * BANK, :]
-                .rearrange("g p n t -> p g (n t)")
-                .bitcast(I32),
-            )
-            w_last.append(w_bank)
+        for c0, width, loads in LAST_PIECES:
+            w_piece = const.tile([P, LAST_GROUPS, width], U32, name="w_piece%d" % c0, align_bytes=64)
+            done = 0
+            for count in loads:
+                nc.sync.dma_start(
+                    out=w_piece[:, done : done + count, :].bitcast(I32),
+                    in_=w_words[first_last + done : first_last + done + count, :, c0 : c0 + width, :]
+                    .rearrange("g p n t -> p g (n t)")
+                    .bitcast(I32),
+                )
+                done += count
+            w_last.append((c0, width, w_piece))
 
         rotated = const.tile([P, N], F32)
         heads_stored = 0
-        for bank in range(BANKS):
-            for j in range(LAST_GROUPS):
-                mx_pass(first_last + j, bank, w_last[bank][:, j, :])
 
-            t0 = bank * BLOCK
+        def rotate(unit):
+            c0, width = UNITS[unit]
+            t0 = c0 // BLOCK % AXES * BLOCK
             by_half = "p (k h i) -> p k h i"
-            acc_halves = acc[bank][:].rearrange(by_half, h=2, i=HALF)
-            sin_halves = sin_flat[:, t0 : t0 + BANK].rearrange(by_half, h=2, i=HALF)
+            acc_halves = acc[unit][:, :width].rearrange(by_half, h=2, i=HALF)
+            sin_halves = sin_flat[:, t0 : t0 + width].rearrange(by_half, h=2, i=HALF)
             own = rope_pool.tile([P, BANK], F32)
             partner = rope_pool.tile([P, BANK], F32)
-            partner_halves = partner[:].rearrange(by_half, h=2, i=HALF)
-            nc.vector.tensor_mul(out=own[:], in0=acc[bank][:], in1=cos_flat[:, t0 : t0 + BANK])
+            partner_halves = partner[:, :width].rearrange(by_half, h=2, i=HALF)
             for h in range(2):
                 nc.vector.tensor_mul(
                     out=partner_halves[:, :, h, :], in0=acc_halves[:, :, 1 - h, :], in1=sin_halves[:, :, h, :]
                 )
-            nc.vector.tensor_add(out=rotated[:, bank * BANK : (bank + 1) * BANK], in0=own[:], in1=partner[:])
+            nc.vector.tensor_mul(out=own[:, :width], in0=acc[unit][:, :width], in1=cos_flat[:, t0 : t0 + width])
+            adder = nc.vector if unit == len(UNITS) - 1 else nc.gpsimd
+            adder.tensor_tensor(out=rotated[:, c0 : c0 + width], in0=own[:, :width], in1=partner[:, :width], op=ALU.add)
 
-            heads_done = (bank + 1) * BANK // HEAD_DIM
-            for b in range(BATCH):
-                rows = slice(b * TOKENS_PER_BATCH, (b + 1) * TOKENS_PER_BATCH)
-                nc.scalar.dma_start(
-                    out=out[b, heads_stored:heads_done].rearrange("h l d -> l h d"),
-                    in_=rotated[rows, heads_stored * HEAD_DIM : heads_done * HEAD_DIM].rearrange(
-                        "l (h d) -> l h d", d=HEAD_DIM
-                    ),
-                )
-            heads_stored = heads_done
+        for c0, width, w_piece in w_last:
+            units = [unit for unit in range(len(UNITS)) if c0 <= UNITS[unit][0] < c0 + width]
+            for j in range(LAST_GROUPS):
+                for unit in units:
+                    u0, u_width = UNITS[unit]
+                    mx_pass(first_last + j, unit, w_piece[:, j, u0 - c0 : u0 - c0 + u_width])
+            for unit in units:
+                rotate(unit)
+                heads_done = sum(UNITS[unit]) // HEAD_DIM
+                for b in range(BATCH):
+                    rows = slice(b * TOKENS_PER_BATCH, (b + 1) * TOKENS_PER_BATCH)
+                    nc.sync.dma_start(
+                        out=out[b, heads_stored:heads_done].rearrange("h l d -> l h d"),
+                        in_=rotated[rows, heads_stored * HEAD_DIM : heads_done * HEAD_DIM].rearrange(
+                            "l (h d) -> l h d", d=HEAD_DIM
+                        ),
+                    )
+                heads_stored = heads_done

@@ -33,8 +33,20 @@ PLANES_PER_TILE = 4
 QUADS = GROUPS // PLANES_PER_TILE
 LAST_GROUPS = 8
 UNITS = ((0, 512), (512, 512), (1024, 256), (1280, 256))
-LAST_PIECES = ((0, 1024, (2, 2, 2, 1, 1)), (1024, 256, (4, 4)), (1280, 256, (4, 3, 1)))
-W_BUFS = 8
+LAST_LOADS = (
+    (0, 1024, 0, 2),
+    (0, 1024, 2, 2),
+    (0, 1024, 4, 2),
+    (0, 1024, 6, 1),
+    (0, 1024, 7, 1),
+    (1024, 512, 0, 3),
+    (1024, 512, 3, 2),
+    (1024, 256, 5, 3),
+    (1280, 256, 5, 2),
+    (1280, 256, 7, 1),
+)
+FRONT_QUADS = 2
+W_BUFS = 13
 TABLE_REPEATS = 6
 
 FLOPS = 2 * P * K * N
@@ -65,16 +77,16 @@ def tile_crossattnrope_pa_k_kernel(tc, x_in, coords, w_words, w_scales, out):
 
         w_planes = const.tile([P, QUADS, N], U8, align_bytes=64)
         nc.vector.memset(w_planes[:].rearrange("p u n -> p (u n)").bitcast(I32), 0)
-        for quad in range(QUADS):
-            g0 = quad * PLANES_PER_TILE
-            for quarter in range(4):
-                nc.sync.dma_start(
-                    out=w_planes[32 * quarter : 32 * quarter + 16, quad, :].bitcast(I32),
-                    in_=w_scales[g0 : g0 + PLANES_PER_TILE, 4 * quarter : 4 * quarter + 4, :].bitcast(I32),
-                )
-
         identity = const.tile([P, P], F32)
         make_identity(nc, identity[:])
+        for quad in range(QUADS):
+            g0 = quad * PLANES_PER_TILE
+            queue, word = (nc.sync, I32) if quad < FRONT_QUADS else (nc.gpsimd, F32)
+            for quarter in range(4):
+                queue.dma_start(
+                    out=w_planes[32 * quarter : 32 * quarter + 16, quad, :].bitcast(word),
+                    in_=w_scales[g0 : g0 + PLANES_PER_TILE, 4 * quarter : 4 * quarter + 4, :].bitcast(word),
+                )
 
         angle = const.tile([P, 2, AXES, HALF], F32)
         for i in range(HALF):
@@ -169,19 +181,13 @@ def tile_crossattnrope_pa_k_kernel(tc, x_in, coords, w_words, w_scales, out):
             for unit, (c0, width) in enumerate(UNITS):
                 mx_pass(group, unit, w_group[:, c0 : c0 + width])
 
-        w_last = []
-        for c0, width, loads in LAST_PIECES:
-            w_piece = const.tile([P, LAST_GROUPS, width], U32, name="w_piece%d" % c0, align_bytes=64)
-            done = 0
-            for count in loads:
-                nc.sync.dma_start(
-                    out=w_piece[:, done : done + count, :].bitcast(I32),
-                    in_=w_words[first_last + done : first_last + done + count, :, c0 : c0 + width, :]
-                    .rearrange("g p n t -> p g (n t)")
-                    .bitcast(I32),
-                )
-                done += count
-            w_last.append((c0, width, w_piece))
+        w_last = const.tile([P, LAST_GROUPS, N], U32, align_bytes=64)
+        for c0, width, first, count in LAST_LOADS:
+            group = first_last + first
+            nc.sync.dma_start(
+                out=w_last[:, first : first + count, c0 : c0 + width].bitcast(I32),
+                in_=w_words[group : group + count, :, c0 : c0 + width, :].rearrange("g p n t -> p g (n t)").bitcast(I32),
+            )
 
         rotated = const.tile([P, N], F32)
         heads_stored = 0
@@ -200,16 +206,21 @@ def tile_crossattnrope_pa_k_kernel(tc, x_in, coords, w_words, w_scales, out):
                     out=partner_halves[:, :, h, :], in0=acc_halves[:, :, 1 - h, :], in1=sin_halves[:, :, h, :]
                 )
             nc.vector.tensor_mul(out=own[:, :width], in0=acc[unit][:, :width], in1=cos_flat[:, t0 : t0 + width])
-            adder = nc.vector if unit == len(UNITS) - 1 else nc.gpsimd
+            adder = nc.gpsimd if unit < 2 else nc.vector
             adder.tensor_tensor(out=rotated[:, c0 : c0 + width], in0=own[:, :width], in1=partner[:, :width], op=ALU.add)
 
-        for c0, width, w_piece in w_last:
-            units = [unit for unit in range(len(UNITS)) if c0 <= UNITS[unit][0] < c0 + width]
-            for j in range(LAST_GROUPS):
+        split = LAST_GROUPS - 3
+        for units, first, end, complete in (
+            ((0, 1), 0, LAST_GROUPS, (0, 1)),
+            ((2, 3), 0, split, ()),
+            ((2,), split, LAST_GROUPS, (2,)),
+            ((3,), split, LAST_GROUPS, (3,)),
+        ):
+            for j in range(first, end):
                 for unit in units:
-                    u0, u_width = UNITS[unit]
-                    mx_pass(first_last + j, unit, w_piece[:, j, u0 - c0 : u0 - c0 + u_width])
-            for unit in units:
+                    c0, width = UNITS[unit]
+                    mx_pass(first_last + j, unit, w_last[:, j, c0 : c0 + width])
+            for unit in complete:
                 rotate(unit)
                 heads_done = sum(UNITS[unit]) // HEAD_DIM
                 for b in range(BATCH):

import math
from contextlib import ExitStack

import concourse.mybir as mybir
from concourse.masks import make_identity

F32 = mybir.dt.float32
BF16 = mybir.dt.bfloat16
I32 = mybir.dt.int32
U32 = mybir.dt.uint32
U8 = mybir.dt.uint8
FP8X4 = mybir.dt.float8_e4m3fn_x4
ALU = mybir.AluOpType
ACT = mybir.ActivationFunctionType

P = 128
BATCH, TOKENS_PER_BATCH = 2, 64
K = 16384
K_PASS = 512
GROUPS = K // K_PASS
HEADS, HEAD_DIM, AXES = 16, 96, 3
BLOCK = HEAD_DIM // AXES
HALF = BLOCK // 2
N = HEADS * HEAD_DIM
BANK = 512
ROPE_BASE = 10000.0

X_CHUNK_GROUPS = 8
X_CHUNKS = GROUPS // X_CHUNK_GROUPS
WORDS_PER_GROUP = K_PASS // 2
QUANT_GROUPS = 4
PLANES_PER_TILE = 4
QUADS = GROUPS // PLANES_PER_TILE
LAST_GROUPS = 8
UNITS = ((0, 512), (512, 512), (1024, 256), (1280, 256))
LAST_LOADS = (
    (0, 1024, 0, 2),
    (0, 1024, 2, 2),
    (0, 1024, 4, 2),
    (0, 1024, 6, 1),
    (0, 1024, 7, 1),
    (1024, 512, 0, 3),
    (1024, 512, 3, 2),
    (1024, 256, 5, 3),
    (1280, 256, 5, 2),
    (1280, 256, 7, 1),
)
FRONT_QUADS = 2
W_BUFS = 13
TABLE_REPEATS = 6

FLOPS = 2 * P * K * N


def tile_crossattnrope_pa_k_kernel(tc, x_in, coords, w_words, w_scales, out):
    nc = tc.nc
    x_rows = x_in.rearrange("b l k -> (b l) k")

    with ExitStack() as stack:
        const = stack.enter_context(tc.tile_pool(name="const", bufs=1))
        x_pool = stack.enter_context(tc.tile_pool(name="x_pool", bufs=X_CHUNKS))
        grouped_pool = stack.enter_context(tc.tile_pool(name="grouped_pool", bufs=3))
        w_pool = stack.enter_context(tc.tile_pool(name="w_pool", bufs=W_BUFS))
        rope_pool = stack.enter_context(tc.tile_pool(name="rope_pool", bufs=len(UNITS)))
        acc_pool = stack.enter_context(tc.psum_pool(name="acc_pool", bufs=1))
        xt_pool = stack.enter_context(tc.psum_pool(name="xt_pool", bufs=4))
        stack.enter_context(tc.manual_schedule())

        x_chunks = []
        for chunk in range(X_CHUNKS):
            x_sb = x_pool.tile([P, X_CHUNK_GROUPS * K_PASS], BF16, name="x_sb")
            k0 = chunk * X_CHUNK_GROUPS * K_PASS
            nc.sync.dma_start(out=x_sb[:], in_=x_rows[:, k0 : k0 + X_CHUNK_GROUPS * K_PASS])
            x_chunks.append(x_sb)
        coords_sb = const.tile([P, AXES], BF16)
        nc.scalar.dma_start(out=coords_sb[:], in_=coords.rearrange("b l a -> (b l) a"))

        w_planes = const.tile([P, QUADS, N], U8, align_bytes=64)
        nc.vector.memset(w_planes[:].rearrange("p u n -> p (u n)").bitcast(I32), 0)
        identity = const.tile([P, P], F32)
        make_identity(nc, identity[:])
        for quad in range(QUADS):
            g0 = quad * PLANES_PER_TILE
            queue, word = (nc.sync, I32) if quad < FRONT_QUADS else (nc.gpsimd, F32)
            for quarter in range(4):
                queue.dma_start(
                    out=w_planes[32 * quarter : 32 * quarter + 16, quad, :].bitcast(word),
                    in_=w_scales[g0 : g0 + PLANES_PER_TILE, 4 * quarter : 4 * quarter + 4, :].bitcast(word),
                )

        angle = const.tile([P, 2, AXES, HALF], F32)
        for i in range(HALF):
            nc.vector.tensor_scalar(
                out=angle[:, 1, :, i], in0=coords_sb[:], scalar1=ROPE_BASE ** (-i / HALF), scalar2=None, op0=ALU.mult
            )
        nc.vector.tensor_scalar_add(out=angle[:, 0], in0=angle[:, 1], scalar1=math.pi / 2)
        angle_flat = angle[:].rearrange("p s a i -> p (s a i)")
        turns_int = const.tile([P, 2 * AXES * HALF], I32)
        nc.vector.tensor_scalar(
            out=turns_int[:], in0=angle_flat, scalar1=1.0 / (2 * math.pi), scalar2=None, op0=ALU.mult
        )
        turns = const.tile([P, 2 * AXES * HALF], F32)
        nc.vector.tensor_copy(out=turns[:], in_=turns_int[:])
        reduced = const.tile([P, 2 * AXES * HALF], F32)
        nc.vector.scalar_tensor_tensor(
            out=reduced[:], in0=turns[:], scalar=-2 * math.pi, in1=angle_flat, op0=ALU.mult, op1=ALU.add
        )
        above = const.tile([P, 2 * AXES * HALF], F32)
        nc.vector.tensor_scalar(
            out=above[:], in0=reduced[:], scalar1=math.pi, scalar2=-2 * math.pi, op0=ALU.is_gt, op1=ALU.mult
        )
        below = const.tile([P, 2 * AXES * HALF], F32)
        nc.vector.tensor_scalar(
            out=below[:], in0=reduced[:], scalar1=-math.pi, scalar2=2 * math.pi, op0=ALU.is_lt, op1=ALU.mult
        )
        nc.vector.tensor_add(out=above[:], in0=above[:], in1=below[:])
        wrapped = const.tile([P, 2, AXES, HALF], F32)
        nc.vector.tensor_add(out=wrapped[:].rearrange("p s a i -> p (s a i)"), in0=reduced[:], in1=above[:])

        cos_table = const.tile([P, TABLE_REPEATS, AXES, 2, HALF], F32)
        sin_table = const.tile([P, TABLE_REPEATS, AXES, 2, HALF], F32)
        table_shape = [P, TABLE_REPEATS, AXES, HALF]
        for_cos = wrapped[:, 0].unsqueeze(1).to_broadcast(table_shape)
        for_sin = wrapped[:, 1].unsqueeze(1).to_broadcast(table_shape)
        nc.scalar.activation(out=cos_table[:, :, :, 0, :], in_=for_cos, func=ACT.Sin)
        nc.scalar.activation(out=cos_table[:, :, :, 1, :], in_=for_cos, func=ACT.Sin)
        nc.scalar.activation(out=sin_table[:, :, :, 0, :], in_=for_sin, func=ACT.Sin, scale=-1.0)
        nc.scalar.activation(out=sin_table[:, :, :, 1, :], in_=for_sin, func=ACT.Sin)
        cos_flat = cos_table[:].rearrange("p r a h i -> p (r a h i)")
        sin_flat = sin_table[:].rearrange("p r a h i -> p (r a h i)")

        x_codes = const.tile([P, GROUPS * P], U32, align_bytes=64)
        x_scales = const.tile([P, GROUPS * P], U8, align_bytes=64)
        groups_per_bank = BANK // (2 * P)
        for chunk in range(X_CHUNKS):
            x_words = x_chunks[chunk][:].bitcast(F32)
            for call in range(X_CHUNK_GROUPS // QUANT_GROUPS):
                grouped = grouped_pool.tile([P, QUANT_GROUPS * P * 4], BF16, align_bytes=64)
                grouped_words = grouped[:].bitcast(F32)
                for bank in range(QUANT_GROUPS // groups_per_bank):
                    xt = xt_pool.tile([P, groups_per_bank, 2, P], F32)
                    for j in range(groups_per_bank):
                        w0 = ((call * QUANT_GROUPS) + bank * groups_per_bank + j) * WORDS_PER_GROUP
                        for u in range(2):
                            nc.tensor.transpose(
                                xt[:, j, u, :], x_words[:, w0 + u : w0 + WORDS_PER_GROUP : 2], identity[:]
                            )
                    side_by_side = grouped_words[:, bank * BANK : (bank + 1) * BANK].rearrange(
                        "p (j r u) -> p j r u", j=groups_per_bank, u=2
                    )
                    if call == 0 and bank == 0:
                        nc.vector.tensor_copy(out=side_by_side, in_=xt[:].rearrange("p j u r -> p j r u"))
                    else:
                        nc.scalar.copy(out=side_by_side, in_=xt[:].rearrange("p j u r -> p j r u"))
                c0 = (chunk * X_CHUNK_GROUPS + call * QUANT_GROUPS) * P
                nc.vector.quantize_mx(
                    out=x_codes[:, c0 : c0 + QUANT_GROUPS * P].bitcast(FP8X4),
                    scales=x_scales[:, c0 : c0 + QUANT_GROUPS * P],
                    in_=grouped[:],
                )

        acc = [acc_pool.tile([P, BANK], F32, name="acc%d" % unit) for unit in range(len(UNITS))]

        def mx_pass(group, unit, w_codes):
            quad, plane = divmod(group, PLANES_PER_TILE)
            c0, width = UNITS[unit]
            nc.tensor.matmul_mx(
                out=acc[unit][:, :width],
                lhsT=x_codes[:, group * P : (group + 1) * P].bitcast(FP8X4),
                lhsT_scale=x_scales[:, group * P : (group + 1) * P],
                rhs=w_codes.bitcast(FP8X4),
                rhs_scale=w_planes[4 * plane : P, quad, c0 : c0 + width],
                start=(group == 0),
                stop=(group == GROUPS - 1),
            )

        first_last = GROUPS - LAST_GROUPS
        for group in range(first_last):
            w_group = w_pool.tile([P, N], U32, align_bytes=64)
            nc.sync.dma_start(out=w_group[:].bitcast(I32), in_=w_words[group].rearrange("p n t -> p (n t)").bitcast(I32))
            for unit, (c0, width) in enumerate(UNITS):
                mx_pass(group, unit, w_group[:, c0 : c0 + width])

        w_last = const.tile([P, LAST_GROUPS, N], U32, align_bytes=64)
        for c0, width, first, count in LAST_LOADS:
            group = first_last + first
            nc.sync.dma_start(
                out=w_last[:, first : first + count, c0 : c0 + width].bitcast(I32),
                in_=w_words[group : group + count, :, c0 : c0 + width, :].rearrange("g p n t -> p g (n t)").bitcast(I32),
            )

        rotated = const.tile([P, N], F32)
        heads_stored = 0

        def rotate(unit):
            c0, width = UNITS[unit]
            t0 = c0 // BLOCK % AXES * BLOCK
            by_half = "p (k h i) -> p k h i"
            acc_halves = acc[unit][:, :width].rearrange(by_half, h=2, i=HALF)
            sin_halves = sin_flat[:, t0 : t0 + width].rearrange(by_half, h=2, i=HALF)
            own = rope_pool.tile([P, BANK], F32)
            partner = rope_pool.tile([P, BANK], F32)
            partner_halves = partner[:, :width].rearrange(by_half, h=2, i=HALF)
            for h in range(2):
                nc.vector.tensor_mul(
                    out=partner_halves[:, :, h, :], in0=acc_halves[:, :, 1 - h, :], in1=sin_halves[:, :, h, :]
                )
            nc.vector.tensor_mul(out=own[:, :width], in0=acc[unit][:, :width], in1=cos_flat[:, t0 : t0 + width])
            adder = nc.gpsimd if unit < 2 else nc.vector
            adder.tensor_tensor(out=rotated[:, c0 : c0 + width], in0=own[:, :width], in1=partner[:, :width], op=ALU.add)

        split = LAST_GROUPS - 3
        for units, first, end, complete in (
            ((0, 1), 0, LAST_GROUPS, (0, 1)),
            ((2, 3), 0, split, ()),
            ((2,), split, LAST_GROUPS, (2,)),
            ((3,), split, LAST_GROUPS, (3,)),
        ):
            for j in range(first, end):
                for unit in units:
                    c0, width = UNITS[unit]
                    mx_pass(first_last + j, unit, w_last[:, j, c0 : c0 + width])
            for unit in complete:
                rotate(unit)
                heads_done = sum(UNITS[unit]) // HEAD_DIM
                for b in range(BATCH):
                    rows = slice(b * TOKENS_PER_BATCH, (b + 1) * TOKENS_PER_BATCH)
                    nc.sync.dma_start(
                        out=out[b, heads_stored:heads_done].rearrange("h l d -> l h d"),
                        in_=rotated[rows, heads_stored * HEAD_DIM : heads_done * HEAD_DIM].rearrange(
                            "l (h d) -> l h d", d=HEAD_DIM
                        ),
                    )
                heads_stored = heads_done
